import numpy as np
import ml_dtypes


def mxq(x, axis, fmt="e4m3"):
    dtype, down = {"e4m3": (ml_dtypes.float8_e4m3fn, 7), "e5m2": (ml_dtypes.float8_e5m2, 14)}[fmt]
    v = np.moveaxis(np.asarray(x, np.float32).astype(ml_dtypes.bfloat16).astype(np.float64), axis, -1)
    blocks = v.reshape(v.shape[:-1] + (-1, 32))
    amax = np.abs(blocks).max(-1, keepdims=True)
    byte = np.maximum(np.where(amax > 0, np.frexp(amax)[1] - 1 + 127, 0) - down, 1)
    scale = np.exp2(byte - 127.0)
    codes = (blocks / scale).astype(np.float32).astype(dtype).astype(np.float64)
    return np.moveaxis((codes * scale).reshape(v.shape), -1, axis)


WIDE = False


def mx_kscale(k):
    if not WIDE:
        return np.ones(k)
    levels = np.array([10, -10, 5, -5, 0])
    if k % 512:
        return np.exp2(np.random.permutation(np.resize(levels, k // 32))).repeat(32)
    a = np.empty((k // 512, 16))
    for p in range(k // 512):
        a[p, :8] = np.random.permutation(np.resize(levels, 8))
        for g in range(8):
            far = levels[np.abs(levels - a[p, g]) >= 10]
            a[p, g + 8] = far[np.random.randint(len(far))]
    return np.exp2(a.ravel()).repeat(32)


BF16 = ml_dtypes.bfloat16


def bf(x):
    return np.asarray(x, np.float32).astype(BF16)


def f64(x):
    return np.asarray(x).astype(np.float64)


B, T, D, H = 1, 512, 2048, 16
HD = D // H
SCALE = HD ** (-0.5)


def rotate_half(u):
    u1, u2 = np.split(u, 2, axis=-1)
    return np.concatenate([-u2, u1], axis=-1)


def apply_rope(u, sin, cos):
    return u * cos[None, :, None, :] + rotate_half(u) * sin[None, :, None, :]


def draw0():
    s = mx_kscale(D)
    return {"x": bf(np.random.standard_normal((B, T, D)) * s),
            "sin": bf(np.random.standard_normal((T, HD))),
            "cos": bf(np.random.standard_normal((T, HD))),
            "W_qkv": bf(np.random.standard_normal((D, D + 2 * HD)) * 2.0 / np.sqrt(D) / s[:, None])}


def core(x, sin, cos, W_qkv):
    sin, cos = f64(sin), f64(cos)
    qkv = mxq(f64(x), 2, "e4m3") @ mxq(f64(W_qkv), 0, "e4m3")
    q, k, v = np.split(qkv, [D, D + HD], axis=-1)
    q = q.reshape(B, T, H, HD) * SCALE
    q_rot = np.ascontiguousarray(apply_rope(q, sin, cos).transpose(0, 2, 1, 3))
    k_rot = apply_rope(k[:, :, None, :], sin, cos)[:, :, 0, :]
    return q_rot, k_rot, v


def e4m3fn_bytes(y):
    return np.clip(np.asarray(y, np.float64), -448.0, 448.0).astype(np.float32).astype(ml_dtypes.float8_e4m3fn).view(np.uint8)


def e4m3fn_values(b):
    return np.asarray(b, np.uint8).view(ml_dtypes.float8_e4m3fn).astype(np.float64)


def setup_inputs():
    d = draw0()
    x0 = np.asarray(d['W_qkv']).astype(np.float64)
    s = (np.max(np.abs(x0), axis=(1,), keepdims=True) / 448.0).astype(np.float32)
    out = {}
    for k, v in d.items():
        if k == 'W_qkv':
            out['W_qkv_bytes'] = e4m3fn_bytes(x0 / s.astype(np.float64))
            out['W_qkv_scale'] = s
        else:
            out[k] = v
    return out


def reference(x, sin, cos, W_qkv_bytes, W_qkv_scale):
    return core(x, sin, cos, e4m3fn_values(W_qkv_bytes) * W_qkv_scale.astype(np.float64))

@@ -1,0 +1,285 @@
+from contextlib import ExitStack
+
+import concourse.mybir as mybir
+from concourse.masks import make_identity
+
+F32 = mybir.dt.float32
+BF16 = mybir.dt.bfloat16
+U32 = mybir.dt.uint32
+U8 = mybir.dt.uint8
+FP8 = mybir.dt.float8_e4m3fn
+FP8X4 = mybir.dt.float8_e4m3fn_x4
+ALU = mybir.AluOpType
+ACT = mybir.ActivationFunctionType
+
+T = 512
+D = 2048
+HD = 128
+HALF = 64
+NQKV = D + 2 * HD
+SCALE = HD ** (-0.5)
+P = 128
+PACK = 4
+K_PASS = P * PACK
+PASSES = D // K_PASS
+M_TILES = T // P
+FLOPS = 2 * T * D * NQKV
+
+BLOCKS = [(0, 512), (512, 512), (1024, 512), (1536, 512), (2048, 256)]
+GPSIMD_ADDS = set()
+SCALAR_INTERLEAVES = {6, 8, 10, 12, 14, 15, 16, 17, 18, 19}
+VECTOR_WIDENS = {(0, 2), (0, 3)}
+XCOPY = "VVVVVVVV"
+LOOKAHEAD = 4
+FAST_PATTERN = False
+LOAD_ORDER = [("w", 0), ("w", 1), ("x", 0), ("w", 2), ("x", 1), ("w", 3), ("x", 2), ("x", 3)]
+
+
+def tile_multiqueryattention_pa_kernel(tc, x, sin, cos, W_qkv_bytes, W_qkv_scale, out_0, out_1, out_2):
+    nc = tc.nc
+    with ExitStack() as ctx:
+        consts = ctx.enter_context(tc.tile_pool(name="consts", bufs=1))
+        keep = ctx.enter_context(tc.tile_pool(name="keep", bufs=1))
+        widep = ctx.enter_context(tc.tile_pool(name="widep", bufs=8))
+        grpp = ctx.enter_context(tc.tile_pool(name="grpp", bufs=6))
+        epi = ctx.enter_context(tc.tile_pool(name="epi", bufs=6))
+        psum = ctx.enter_context(tc.psum_pool(name="psum", bufs=4))
+        ctx.enter_context(tc.manual_schedule())
+
+        steps = [(b, g) for b in range(len(BLOCKS)) for g in range(PASSES)]
+        n = len(steps)
+
+        warm = consts.tile([P, 2], F32, name="warm")
+        nc.vector.memset(warm[:, 0:1], 0.0)
+        nc.scalar.activation(out=warm[:, 1:2], in_=warm[:, 0:1], func=ACT.Copy)
+
+        ident = consts.tile([P, P], F32, name="ident")
+        make_identity(nc, ident[:])
+
+        wsc = consts.tile([P, PASSES, PACK], F32, name="wsc")
+        nc.sync.dma_start(out=wsc[:], in_=W_qkv_scale.rearrange("(g p t) o -> p g (t o)", p=P, t=PACK))
+        wbytes = {}
+        x_sb = {}
+        cos_sb = consts.tile([P, M_TILES, HD], BF16, name="cos_sb")
+        sin_sb = consts.tile([P, M_TILES, HD], BF16, name="sin_sb")
+
+        def load_w(b, g):
+            c0, w = BLOCKS[b]
+            wb = keep.tile([P, PACK, w], U8, name="wbytes%d_%d" % (b, g))
+            nc.sync.dma_start(
+                out=wb[:],
+                in_=W_qkv_bytes[g * K_PASS:(g + 1) * K_PASS, c0:c0 + w].rearrange("(p t) n -> p t n", t=PACK),
+            )
+            wbytes[(b, g)] = wb
+
+        def load_x(m):
+            xs = keep.tile([P, D], BF16, name="x_sb%d" % m)
+            nc.sync.dma_start(out=xs[:], in_=x[0, m * P:(m + 1) * P, :])
+            x_sb[m] = xs
+
+        for item in LOAD_ORDER:
+            if item[0] == "w":
+                load_w(0, item[1])
+            else:
+                load_x(item[1])
+        for b in range(1, len(BLOCKS)):
+            for g in range(PASSES):
+                load_w(b, g)
+            if b == 1:
+                nc.sync.dma_start(out=cos_sb[:], in_=cos.rearrange("(m p) j -> p m j", p=P))
+                nc.sync.dma_start(out=sin_sb[:], in_=sin.rearrange("(m p) j -> p m j", p=P))
+
+        wide_t = {}
+        grp_t = {}
+        codes_t = {}
+        state = {"widened": 0}
+
+        def widen(s):
+            b, g = steps[s]
+            w = BLOCKS[b][1]
+            wide = widep.tile([P, PACK, w], BF16, tag="wide")
+            for t in range(PACK):
+                src = wbytes[(b, g)][:, t, :].bitcast(FP8)
+                if (s, t) in VECTOR_WIDENS:
+                    nc.vector.tensor_scalar(out=wide[:, t, :], in0=src, scalar1=wsc[:, g, t:t + 1], scalar2=None, op0=ALU.mult)
+                else:
+                    nc.scalar.activation(out=wide[:, t, :], in_=src, func=ACT.Copy, scale=wsc[:, g, t:t + 1])
+            wide_t[s] = wide
+
+        def do_interleave(s):
+            b, g = steps[s]
+            w = BLOCKS[b][1]
+            grp = grpp.tile([P, w, PACK], BF16, tag="grp", align_bytes=64)
+            if FAST_PATTERN:
+                dst = grp[:].rearrange("p (c i) t -> p c t i", i=4)
+                src = wide_t[s][:].rearrange("p t (c i) -> p c t i", i=4)
+            else:
+                dst = grp[:]
+                src = wide_t[s][:].rearrange("p t n -> p n t")
+            if s in SCALAR_INTERLEAVES:
+                nc.scalar.copy(out=dst, in_=src)
+            else:
+                nc.vector.tensor_copy(out=dst, in_=src)
+            grp_t[s] = grp
+
+        def widen_to(k):
+            while state["widened"] < min(k, n):
+                s = state["widened"]
+                widen(s)
+                state["widened"] = s + 1
+                if s in SCALAR_INTERLEAVES:
+                    do_interleave(s)
+
+        def interleave(s):
+            if s < n and s not in grp_t:
+                widen_to(s + LOOKAHEAD)
+                if s not in grp_t:
+                    do_interleave(s)
+
+        def quantize(s):
+            b, g = steps[s]
+            w = BLOCKS[b][1]
+            codes = keep.tile([P, w], U32, name="wcodes%d" % s, align_bytes=64)
+            scl = keep.tile([P, w], U8, name="wscl%d" % s, align_bytes=64)
+            nc.vector.quantize_mx(
+                out=codes[:].bitcast(FP8X4),
+                scales=scl[:],
+                in_=grp_t[s][:].rearrange("p n t -> p (n t)"),
+            )
+            codes_t[s] = (codes, scl)
+
+        xt_t = {}
+        xg_t = {}
+        x_codes = {}
+        for m in range(M_TILES):
+            words = x_sb[m][:].bitcast(F32)
+            for gp in range(PASSES // 2):
+                xt = psum.tile([P, 512], F32, tag="xt")
+                for gg in range(2):
+                    g = 2 * gp + gg
+                    for u in range(2):
+                        col = (2 * gg + u) * P
+                        nc.tensor.transpose(xt[:, col:col + P], words[:, 256 * g + u:256 * (g + 1):2], ident[:])
+                xt_t[(m, gp)] = xt
+
+        def xcopy(m, gp):
+            if gp == 0:
+                xg = keep.tile([P, PASSES, P, PACK], BF16, name="xg%d" % m, align_bytes=64)
+                xg_t[m] = xg
+            dst = xg_t[m][:, 2 * gp:2 * gp + 2, :, :].bitcast(F32)
+            src = xt_t[(m, gp)][:].rearrange("p (g u r) -> p g r u", g=2, u=2)
+            if XCOPY[2 * m + gp] == "S":
+                nc.scalar.copy(out=dst, in_=src)
+            else:
+                nc.vector.tensor_copy(out=dst, in_=src)
+
+        def xquant(m):
+            xc = keep.tile([P, PASSES * P], U32, name="xc%d" % m, align_bytes=64)
+            xsc = keep.tile([P, PASSES * P], U8, name="xsc%d" % m, align_bytes=64)
+            nc.vector.quantize_mx(out=xc[:].bitcast(FP8X4), scales=xsc[:], in_=xg_t[m][:].rearrange("p g r t -> p (g r t)"))
+            x_codes[m] = (xc, xsc)
+
+        banks = {}
+
+        def one_matmul(b, g, m):
+            w = BLOCKS[b][1]
+            codes, scl = codes_t[PASSES * b + g]
+            if g == 0:
+                acc = psum.tile([P, 512], F32, tag="acc")
+                banks[(b, m)] = acc
+            xc, xsc = x_codes[m]
+            nc.tensor.matmul_mx(
+                out=banks[(b, m)][:, 0:w],
+                lhsT=xc[:, g * P:(g + 1) * P].bitcast(FP8X4),
+                lhsT_scale=xsc[:, g * P:(g + 1) * P],
+                rhs=codes[:].bitcast(FP8X4),
+                rhs_scale=scl[:],
+                start=(g == 0),
+                stop=(g == PASSES - 1),
+            )
+
+        def matmuls(s):
+            b, g = steps[s]
+            if b == 0:
+                for m in range(g):
+                    one_matmul(0, g, m)
+                for gq in range(g + 1):
+                    one_matmul(0, gq, g)
+            else:
+                for m in range(M_TILES):
+                    one_matmul(b, g, m)
+
+        def rope(acc, nh, m, factor, t1, t2):
+            u = acc.rearrange("p (h j) -> p h j", h=nh)
+            nc.vector.scalar_tensor_tensor(
+                out=t1, in0=u, scalar=factor,
+                in1=cos_sb[:, m, :].unsqueeze(1).to_broadcast([P, nh, HD]),
+                op0=ALU.mult, op1=ALU.mult,
+            )
+            nc.vector.scalar_tensor_tensor(
+                out=t2[:, :, 0:HALF], in0=u[:, :, HALF:HD], scalar=-factor,
+                in1=sin_sb[:, m, 0:HALF].unsqueeze(1).to_broadcast([P, nh, HALF]),
+                op0=ALU.mult, op1=ALU.mult,
+            )
+            nc.vector.scalar_tensor_tensor(
+                out=t2[:, :, HALF:HD], in0=u[:, :, 0:HALF], scalar=factor,
+                in1=sin_sb[:, m, HALF:HD].unsqueeze(1).to_broadcast([P, nh, HALF]),
+                op0=ALU.mult, op1=ALU.mult,
+            )
+
+        pend = {}
+
+        def products(b, m):
+            acc = banks[(b, m)]
+            if b < 4:
+                t1 = epi.tile([P, 4, HD], F32, tag="t1")
+                t2 = epi.tile([P, 4, HD], F32, tag="t2")
+                rope(acc[:, 0:512], 4, m, SCALE, t1[:], t2[:])
+            else:
+                t1 = epi.tile([P, 1, HD], F32, tag="k1")
+                t2 = epi.tile([P, 1, HD], F32, tag="k2")
+                vv = epi.tile([P, HD], F32, tag="vv")
+                nc.scalar.copy(out=vv[:], in_=acc[:, HD:2 * HD])
+                nc.sync.dma_start(out=out_2[0, m * P:(m + 1) * P, :], in_=vv[:])
+                rope(acc[:, 0:HD], 1, m, 1.0, t1[:], t2[:])
+            pend[(b, m)] = (t1, t2)
+
+        def finish(b, m):
+            t1, t2 = pend[(b, m)]
+            eng = nc.gpsimd if (b, m) in GPSIMD_ADDS else nc.vector
+            eng.tensor_tensor(out=t1[:], in0=t1[:], in1=t2[:], op=ALU.add)
+            if b < 4:
+                nc.sync.dma_start(
+                    out=out_0[0, 4 * b:4 * b + 4, m * P:(m + 1) * P, :].rearrange("h p j -> p h j"),
+                    in_=t1[:],
+                )
+            else:
+                nc.sync.dma_start(out=out_1[0, m * P:(m + 1) * P, :], in_=t1[:, 0, :])
+
+        late = []
+        widen_to(LOOKAHEAD)
+        interleave(0)
+        for s in range(n):
+            b, g = steps[s]
+            interleave(s + 1)
+            if b == 0:
+                xcopy(g, 0)
+                xcopy(g, 1)
+            quantize(s)
+            if b == 0:
+                xquant(g)
+            matmuls(s)
+            if g == PASSES - 1:
+                interleave(s + 2)
+                for m in range(M_TILES):
+                    products(b, m)
+                    if (b, m) in GPSIMD_ADDS:
+                        finish(b, m)
+                    else:
+                        late.append((b, m))
+            elif g == 0:
+                for (bb, mm) in late:
+                    finish(bb, mm)
+                late.clear()
+        for (bb, mm) in late:
+            finish(bb, mm)

@@ -26,12 +26,13 @@ M_TILES = T // P
 FLOPS = 2 * T * D * NQKV
 
 BLOCKS = [(0, 512), (512, 512), (1024, 512), (1536, 512), (2048, 256)]
-GPSIMD_ADDS = set()
-SCALAR_INTERLEAVES = {6, 8, 10, 12, 14, 15, 16, 17, 18, 19}
-VECTOR_WIDENS = {(0, 2), (0, 3)}
+GPSIMD_ADDS = {(0, 0), (0, 1), (0, 2), (1, 0), (1, 1), (1, 2), (2, 0), (2, 1), (2, 2), (3, 0), (3, 1), (3, 2)}
+SCALAR_INTERLEAVES = {6, 10, 14, 15, 17, 18, 19}
+VECTOR_WIDENS = {(0, 0), (0, 2), (0, 3), (1, 1)}
 XCOPY = "VVVVVVVV"
 LOOKAHEAD = 4
 FAST_PATTERN = False
+DELAY = 2
 LOAD_ORDER = [("w", 0), ("w", 1), ("x", 0), ("w", 2), ("x", 1), ("w", 3), ("x", 2), ("x", 3)]
 
 
@@ -43,7 +44,7 @@ def tile_multiqueryattention_pa_kernel(tc, x, sin, cos, W_qkv_bytes, W_qkv_scale
         widep = ctx.enter_context(tc.tile_pool(name="widep", bufs=8))
         grpp = ctx.enter_context(tc.tile_pool(name="grpp", bufs=6))
         epi = ctx.enter_context(tc.tile_pool(name="epi", bufs=6))
-        psum = ctx.enter_context(tc.psum_pool(name="psum", bufs=4))
+        psum = ctx.enter_context(tc.psum_pool(name="psum", bufs=8))
         ctx.enter_context(tc.manual_schedule())
 
         steps = [(b, g) for b in range(len(BLOCKS)) for g in range(PASSES)]
@@ -154,7 +155,7 @@ def tile_multiqueryattention_pa_kernel(tc, x, sin, cos, W_qkv_bytes, W_qkv_scale
         for m in range(M_TILES):
             words = x_sb[m][:].bitcast(F32)
             for gp in range(PASSES // 2):
-                xt = psum.tile([P, 512], F32, tag="xt")
+                xt = psum.tile([P, 512], F32, tag="bank")
                 for gg in range(2):
                     g = 2 * gp + gg
                     for u in range(2):
@@ -185,7 +186,7 @@ def tile_multiqueryattention_pa_kernel(tc, x, sin, cos, W_qkv_bytes, W_qkv_scale
             w = BLOCKS[b][1]
             codes, scl = codes_t[PASSES * b + g]
             if g == 0:
-                acc = psum.tile([P, 512], F32, tag="acc")
+                acc = psum.tile([P, 512], F32, tag="bank")
                 banks[(b, m)] = acc
             xc, xsc = x_codes[m]
             nc.tensor.matmul_mx(
@@ -257,6 +258,20 @@ def tile_multiqueryattention_pa_kernel(tc, x, sin, cos, W_qkv_bytes, W_qkv_scale
                 nc.sync.dma_start(out=out_1[0, m * P:(m + 1) * P, :], in_=t1[:, 0, :])
 
         late = []
+
+        def run(b):
+            for m in range(M_TILES):
+                products(b, m)
+                if (b, m) in GPSIMD_ADDS:
+                    finish(b, m)
+                else:
+                    late.append((b, m))
+
+        def flush_late():
+            for (bb, mm) in late:
+                finish(bb, mm)
+            late.clear()
+
         widen_to(LOOKAHEAD)
         interleave(0)
         for s in range(n):
@@ -266,20 +281,15 @@ def tile_multiqueryattention_pa_kernel(tc, x, sin, cos, W_qkv_bytes, W_qkv_scale
                 xcopy(g, 0)
                 xcopy(g, 1)
             quantize(s)
+            flush_late()
             if b == 0:
                 xquant(g)
             matmuls(s)
-            if g == PASSES - 1:
+            sb = s - DELAY
+            if sb >= 0 and steps[sb][1] == PASSES - 1:
                 interleave(s + 2)
-                for m in range(M_TILES):
-                    products(b, m)
-                    if (b, m) in GPSIMD_ADDS:
-                        finish(b, m)
-                    else:
-                        late.append((b, m))
-            elif g == 0:
-                for (bb, mm) in late:
-                    finish(bb, mm)
-                late.clear()
-        for (bb, mm) in late:
-            finish(bb, mm)
+                run(steps[sb][0])
+        for sb in range(n - DELAY, n):
+            if steps[sb][1] == PASSES - 1:
+                run(steps[sb][0])
+        flush_late()

@@ -31,9 +31,9 @@ SCALAR_INTERLEAVES = {6, 10, 14, 15, 17, 18, 19}
 VECTOR_WIDENS = {(0, 0), (0, 2), (0, 3), (1, 1)}
 XCOPY = "VVVVVVVV"
 LOOKAHEAD = 4
-FAST_PATTERN = False
+FAST_PATTERN = True
 DELAY = 2
-LOAD_ORDER = [("w", 0), ("w", 1), ("x", 0), ("w", 2), ("x", 1), ("w", 3), ("x", 2), ("x", 3)]
+LOAD_ORDER = [("w", 0), ("w", 1), ("x", 0), ("w", 2), ("x", 1), ("tab", 0), ("w", 3), ("x", 2), ("x", 3)]
 
 
 def tile_multiqueryattention_pa_kernel(tc, x, sin, cos, W_qkv_bytes, W_qkv_scale, out_0, out_1, out_2):
@@ -81,14 +81,23 @@ def tile_multiqueryattention_pa_kernel(tc, x, sin, cos, W_qkv_bytes, W_qkv_scale
         for item in LOAD_ORDER:
             if item[0] == "w":
                 load_w(0, item[1])
-            else:
+            elif item[0] == "x":
                 load_x(item[1])
+            else:
+                nc.sync.dma_start(out=cos_sb[:], in_=cos.rearrange("(m p) j -> p m j", p=P))
+                nc.sync.dma_start(out=sin_sb[:], in_=sin.rearrange("(m p) j -> p m j", p=P))
         for b in range(1, len(BLOCKS)):
             for g in range(PASSES):
                 load_w(b, g)
-            if b == 1:
-                nc.sync.dma_start(out=cos_sb[:], in_=cos.rearrange("(m p) j -> p m j", p=P))
-                nc.sync.dma_start(out=sin_sb[:], in_=sin.rearrange("(m p) j -> p m j", p=P))
+
+        tabq = consts.tile([P, M_TILES, 4, HALF], F32, name="tabq")
+        quarters = [(cos_sb, 0, SCALE), (sin_sb, 0, -SCALE), (sin_sb, 1, SCALE), (cos_sb, 1, SCALE)]
+        for qi in range(4):
+            src_t, hf, fac = quarters[qi]
+            nc.gpsimd.tensor_scalar(
+                out=tabq[:, :, qi, :], in0=src_t[:, :, hf * HALF:(hf + 1) * HALF],
+                scalar1=fac, scalar2=0.0, op0=ALU.mult, op1=ALU.add,
+            )
 
         wide_t = {}
         grp_t = {}
@@ -210,52 +219,45 @@ def tile_multiqueryattention_pa_kernel(tc, x, sin, cos, W_qkv_bytes, W_qkv_scale
                 for m in range(M_TILES):
                     one_matmul(b, g, m)
 
-        def rope(acc, nh, m, factor, t1, t2):
-            u = acc.rearrange("p (h j) -> p h j", h=nh)
-            nc.vector.scalar_tensor_tensor(
-                out=t1, in0=u, scalar=factor,
-                in1=cos_sb[:, m, :].unsqueeze(1).to_broadcast([P, nh, HD]),
-                op0=ALU.mult, op1=ALU.mult,
-            )
-            nc.vector.scalar_tensor_tensor(
-                out=t2[:, :, 0:HALF], in0=u[:, :, HALF:HD], scalar=-factor,
-                in1=sin_sb[:, m, 0:HALF].unsqueeze(1).to_broadcast([P, nh, HALF]),
-                op0=ALU.mult, op1=ALU.mult,
-            )
-            nc.vector.scalar_tensor_tensor(
-                out=t2[:, :, HALF:HD], in0=u[:, :, 0:HALF], scalar=factor,
-                in1=sin_sb[:, m, HALF:HD].unsqueeze(1).to_broadcast([P, nh, HALF]),
-                op0=ALU.mult, op1=ALU.mult,
-            )
-
         pend = {}
 
         def products(b, m):
             acc = banks[(b, m)]
             if b < 4:
-                t1 = epi.tile([P, 4, HD], F32, tag="t1")
-                t2 = epi.tile([P, 4, HD], F32, tag="t2")
-                rope(acc[:, 0:512], 4, m, SCALE, t1[:], t2[:])
+                tt = epi.tile([P, 4, 2, HD], F32, tag="tt")
+                nc.vector.tensor_tensor(
+                    out=tt[:],
+                    in0=acc[:, 0:512].rearrange("p (h j) -> p h j", h=4).unsqueeze(2).to_broadcast([P, 4, 2, HD]),
+                    in1=tabq[:, m, :, :].rearrange("p (w r) i -> p w (r i)", w=2).unsqueeze(1).to_broadcast([P, 4, 2, HD]),
+                    op=ALU.mult,
+                )
             else:
-                t1 = epi.tile([P, 1, HD], F32, tag="k1")
-                t2 = epi.tile([P, 1, HD], F32, tag="k2")
+                tt = epi.tile([P, 1, 2, HD], F32, tag="tk")
                 vv = epi.tile([P, HD], F32, tag="vv")
                 nc.scalar.copy(out=vv[:], in_=acc[:, HD:2 * HD])
                 nc.sync.dma_start(out=out_2[0, m * P:(m + 1) * P, :], in_=vv[:])
-                rope(acc[:, 0:HD], 1, m, 1.0, t1[:], t2[:])
-            pend[(b, m)] = (t1, t2)
+                nc.vector.scalar_tensor_tensor(
+                    out=tt[:, 0, :, :],
+                    in0=acc[:, 0:HD].unsqueeze(1).to_broadcast([P, 2, HD]),
+                    scalar=1.0 / SCALE,
+                    in1=tabq[:, m, :, :].rearrange("p (w r) i -> p w (r i)", w=2),
+                    op0=ALU.mult, op1=ALU.mult,
+                )
+            pend[(b, m)] = tt
 
         def finish(b, m):
-            t1, t2 = pend[(b, m)]
+            tt = pend[(b, m)]
+            nh = 4 if b < 4 else 1
+            oo = epi.tile([P, nh, 2, HALF], F32, tag="oq" if b < 4 else "ok")
             eng = nc.gpsimd if (b, m) in GPSIMD_ADDS else nc.vector
-            eng.tensor_tensor(out=t1[:], in0=t1[:], in1=t2[:], op=ALU.add)
+            eng.tensor_tensor(out=oo[:], in0=tt[:, :, :, 0:HALF], in1=tt[:, :, :, HALF:HD], op=ALU.add)
             if b < 4:
                 nc.sync.dma_start(
                     out=out_0[0, 4 * b:4 * b + 4, m * P:(m + 1) * P, :].rearrange("h p j -> p h j"),
-                    in_=t1[:],
+                    in_=oo[:].rearrange("p h w i -> p h (w i)"),
                 )
             else:
-                nc.sync.dma_start(out=out_1[0, m * P:(m + 1) * P, :], in_=t1[:, 0, :])
+                nc.sync.dma_start(out=out_1[0, m * P:(m + 1) * P, :], in_=oo[:].rearrange("p h w i -> p (h w i)"))
 
         late = []
 

@@ -26,7 +26,7 @@ M_TILES = T // P
 FLOPS = 2 * T * D * NQKV
 
 BLOCKS = [(0, 512), (512, 512), (1024, 512), (1536, 512), (2048, 256)]
-GPSIMD_ADDS = {(0, 0), (0, 1), (0, 2), (1, 0), (1, 1), (1, 2), (2, 0), (2, 1), (2, 2), (3, 0), (3, 1), (3, 2)}
+GPSIMD_ADDS = {(0, 0), (0, 1), (1, 0), (1, 1), (2, 0), (2, 1), (3, 0), (3, 1)}
 SCALAR_INTERLEAVES = {6, 10, 14, 15, 17, 18, 19}
 VECTOR_WIDENS = {(0, 0), (0, 2), (0, 3), (1, 1)}
 XCOPY = "VVVVVVVV"

@@ -27,11 +27,11 @@ FLOPS = 2 * T * D * NQKV
 
 BLOCKS = [(0, 512), (512, 512), (1024, 512), (1536, 512), (2048, 256)]
 GPSIMD_ADDS = {(0, 0), (0, 1), (1, 0), (1, 1), (2, 0), (2, 1), (3, 0), (3, 1)}
-SCALAR_INTERLEAVES = {6, 10, 14, 15, 17, 18, 19}
+PE_STEPS = {4, 6, 8, 10, 12, 14, 15}
+S_STEPS = {17, 18, 19}
 VECTOR_WIDENS = {(0, 0), (0, 2), (0, 3), (1, 1)}
-XCOPY = "VVVVVVVV"
 LOOKAHEAD = 4
-FAST_PATTERN = True
+EVAC_LAG = 2
 DELAY = 2
 LOAD_ORDER = [("w", 0), ("w", 1), ("x", 0), ("w", 2), ("x", 1), ("tab", 0), ("w", 3), ("x", 2), ("x", 3)]
 
@@ -44,7 +44,7 @@ def tile_multiqueryattention_pa_kernel(tc, x, sin, cos, W_qkv_bytes, W_qkv_scale
         widep = ctx.enter_context(tc.tile_pool(name="widep", bufs=8))
         grpp = ctx.enter_context(tc.tile_pool(name="grpp", bufs=6))
         epi = ctx.enter_context(tc.tile_pool(name="epi", bufs=6))
-        psum = ctx.enter_context(tc.psum_pool(name="psum", bufs=8))
+        psum = ctx.enter_context(tc.psum_pool(name="psum", bufs=4))
         ctx.enter_context(tc.manual_schedule())
 
         steps = [(b, g) for b in range(len(BLOCKS)) for g in range(PASSES)]
@@ -56,6 +56,8 @@ def tile_multiqueryattention_pa_kernel(tc, x, sin, cos, W_qkv_bytes, W_qkv_scale
 
         ident = consts.tile([P, P], F32, name="ident")
         make_identity(nc, ident[:])
+        identb = consts.tile([P, P], BF16, name="identb")
+        make_identity(nc, identb[:])
 
         wsc = consts.tile([P, PASSES, PACK], F32, name="wsc")
         nc.sync.dma_start(out=wsc[:], in_=W_qkv_scale.rearrange("(g p t) o -> p g (t o)", p=P, t=PACK))
@@ -101,6 +103,7 @@ def tile_multiqueryattention_pa_kernel(tc, x, sin, cos, W_qkv_bytes, W_qkv_scale
 
         wide_t = {}
         grp_t = {}
+        pil_t = {}
         codes_t = {}
         state = {"widened": 0}
 
@@ -116,20 +119,37 @@ def tile_multiqueryattention_pa_kernel(tc, x, sin, cos, W_qkv_bytes, W_qkv_scale
                     nc.scalar.activation(out=wide[:, t, :], in_=src, func=ACT.Copy, scale=wsc[:, g, t:t + 1])
             wide_t[s] = wide
 
-        def do_interleave(s):
+        def copy_interleave(s):
             b, g = steps[s]
             w = BLOCKS[b][1]
             grp = grpp.tile([P, w, PACK], BF16, tag="grp", align_bytes=64)
-            if FAST_PATTERN:
-                dst = grp[:].rearrange("p (c i) t -> p c t i", i=4)
-                src = wide_t[s][:].rearrange("p t (c i) -> p c t i", i=4)
-            else:
-                dst = grp[:]
-                src = wide_t[s][:].rearrange("p t n -> p n t")
-            if s in SCALAR_INTERLEAVES:
+            dst = grp[:].rearrange("p (c i) t -> p c t i", i=4)
+            src = wide_t[s][:].rearrange("p t (c i) -> p c t i", i=4)
+            if s in S_STEPS:
                 nc.scalar.copy(out=dst, in_=src)
             else:
                 nc.vector.tensor_copy(out=dst, in_=src)
+            grp_t[s] = grp
+
+        def pe_interleave(s):
+            halves = []
+            for h in range(2):
+                pil = psum.tile([P, 1024], BF16, tag="pil")
+                for q in range(2):
+                    c0 = (2 * h + q) * P
+                    nc.tensor.matmul(
+                        out=pil[:, q * 512:(q + 1) * 512], lhsT=identb[:],
+                        rhs=wide_t[s][:, :, c0:c0 + P].rearrange("p t c -> p c t"),
+                        start=True, stop=True,
+                    )
+                halves.append(pil)
+            pil_t[s] = halves
+
+        def evacuate(s):
+            grp = grpp.tile([P, 512, PACK], BF16, tag="grp", align_bytes=64)
+            flat = grp[:].rearrange("p n t -> p (n t)")
+            for h in range(2):
+                nc.scalar.copy(out=flat[:, h * 1024:(h + 1) * 1024], in_=pil_t[s][h][:])
             grp_t[s] = grp
 
         def widen_to(k):
@@ -137,14 +157,18 @@ def tile_multiqueryattention_pa_kernel(tc, x, sin, cos, W_qkv_bytes, W_qkv_scale
                 s = state["widened"]
                 widen(s)
                 state["widened"] = s + 1
-                if s in SCALAR_INTERLEAVES:
-                    do_interleave(s)
+                if s in S_STEPS:
+                    copy_interleave(s)
+                if s - EVAC_LAG in PE_STEPS:
+                    evacuate(s - EVAC_LAG)
+                if s in PE_STEPS:
+                    pe_interleave(s)
 
         def interleave(s):
             if s < n and s not in grp_t:
                 widen_to(s + LOOKAHEAD)
                 if s not in grp_t:
-                    do_interleave(s)
+                    copy_interleave(s)
 
         def quantize(s):
             b, g = steps[s]
@@ -161,10 +185,11 @@ def tile_multiqueryattention_pa_kernel(tc, x, sin, cos, W_qkv_bytes, W_qkv_scale
         xt_t = {}
         xg_t = {}
         x_codes = {}
-        for m in range(M_TILES):
+
+        def xtranspose(m):
             words = x_sb[m][:].bitcast(F32)
             for gp in range(PASSES // 2):
-                xt = psum.tile([P, 512], F32, tag="bank")
+                xt = psum.tile([P, 512], F32, tag="acc")
                 for gg in range(2):
                     g = 2 * gp + gg
                     for u in range(2):
@@ -178,10 +203,7 @@ def tile_multiqueryattention_pa_kernel(tc, x, sin, cos, W_qkv_bytes, W_qkv_scale
                 xg_t[m] = xg
             dst = xg_t[m][:, 2 * gp:2 * gp + 2, :, :].bitcast(F32)
             src = xt_t[(m, gp)][:].rearrange("p (g u r) -> p g r u", g=2, u=2)
-            if XCOPY[2 * m + gp] == "S":
-                nc.scalar.copy(out=dst, in_=src)
-            else:
-                nc.vector.tensor_copy(out=dst, in_=src)
+            nc.vector.tensor_copy(out=dst, in_=src)
 
         def xquant(m):
             xc = keep.tile([P, PASSES * P], U32, name="xc%d" % m, align_bytes=64)
@@ -195,7 +217,7 @@ def tile_multiqueryattention_pa_kernel(tc, x, sin, cos, W_qkv_bytes, W_qkv_scale
             w = BLOCKS[b][1]
             codes, scl = codes_t[PASSES * b + g]
             if g == 0:
-                acc = psum.tile([P, 512], F32, tag="bank")
+                acc = psum.tile([P, 512], F32, tag="acc" if b < 4 else "pil")
                 banks[(b, m)] = acc
             xc, xsc = x_codes[m]
             nc.tensor.matmul_mx(
@@ -210,11 +232,11 @@ def tile_multiqueryattention_pa_kernel(tc, x, sin, cos, W_qkv_bytes, W_qkv_scale
 
         def matmuls(s):
             b, g = steps[s]
-            if b == 0:
-                for m in range(g):
-                    one_matmul(0, g, m)
-                for gq in range(g + 1):
-                    one_matmul(0, gq, g)
+            if b < 4:
+                if g == PASSES - 1:
+                    for m in range(M_TILES):
+                        for gq in range(PASSES):
+                            one_matmul(b, gq, m)
             else:
                 for m in range(M_TILES):
                     one_matmul(b, g, m)
@@ -274,6 +296,8 @@ def tile_multiqueryattention_pa_kernel(tc, x, sin, cos, W_qkv_bytes, W_qkv_scale
                 finish(bb, mm)
             late.clear()
 
+        xtranspose(0)
+        xtranspose(1)
         widen_to(LOOKAHEAD)
         interleave(0)
         for s in range(n):
@@ -282,6 +306,8 @@ def tile_multiqueryattention_pa_kernel(tc, x, sin, cos, W_qkv_bytes, W_qkv_scale
             if b == 0:
                 xcopy(g, 0)
                 xcopy(g, 1)
+                if g + 2 < M_TILES:
+                    xtranspose(g + 2)
             quantize(s)
             flush_late()
             if b == 0:

@@ -27,11 +27,12 @@ FLOPS = 2 * T * D * NQKV
 
 BLOCKS = [(0, 512), (512, 512), (1024, 512), (1536, 512), (2048, 256)]
 GPSIMD_ADDS = {(0, 0), (0, 1), (1, 0), (1, 1), (2, 0), (2, 1), (3, 0), (3, 1)}
-PE_STEPS = {4, 6, 8, 10, 12, 14, 15}
+PE_STEPS = {6, 7, 8, 10, 12, 14, 15}
 S_STEPS = {17, 18, 19}
 VECTOR_WIDENS = {(0, 0), (0, 2), (0, 3), (1, 1)}
-LOOKAHEAD = 4
-EVAC_LAG = 2
+LA_W = 4
+LA_P = 4
+LA_E = 2
 DELAY = 2
 LOAD_ORDER = [("w", 0), ("w", 1), ("x", 0), ("w", 2), ("x", 1), ("tab", 0), ("w", 3), ("x", 2), ("x", 3)]
 
@@ -157,18 +158,18 @@ def tile_multiqueryattention_pa_kernel(tc, x, sin, cos, W_qkv_bytes, W_qkv_scale
                 s = state["widened"]
                 widen(s)
                 state["widened"] = s + 1
-                if s in S_STEPS:
-                    copy_interleave(s)
-                if s - EVAC_LAG in PE_STEPS:
-                    evacuate(s - EVAC_LAG)
-                if s in PE_STEPS:
-                    pe_interleave(s)
+
+        def prepare(s):
+            widen_to(s + LA_W + 1)
+            k = s + LA_E
+            if k < n and k in PE_STEPS:
+                evacuate(k)
+            if k < n and k in S_STEPS:
+                copy_interleave(k)
 
         def interleave(s):
             if s < n and s not in grp_t:
-                widen_to(s + LOOKAHEAD)
-                if s not in grp_t:
-                    copy_interleave(s)
+                copy_interleave(s)
 
         def quantize(s):
             b, g = steps[s]
@@ -189,7 +190,7 @@ def tile_multiqueryattention_pa_kernel(tc, x, sin, cos, W_qkv_bytes, W_qkv_scale
         def xtranspose(m):
             words = x_sb[m][:].bitcast(F32)
             for gp in range(PASSES // 2):
-                xt = psum.tile([P, 512], F32, tag="acc")
+                xt = psum.tile([P, 512], F32, tag="pil")
                 for gg in range(2):
                     g = 2 * gp + gg
                     for u in range(2):
@@ -232,14 +233,18 @@ def tile_multiqueryattention_pa_kernel(tc, x, sin, cos, W_qkv_bytes, W_qkv_scale
 
         def matmuls(s):
             b, g = steps[s]
-            if b < 4:
-                if g == PASSES - 1:
-                    for m in range(M_TILES):
-                        for gq in range(PASSES):
-                            one_matmul(b, gq, m)
-            else:
+            if b == 0:
+                for m in range(g):
+                    one_matmul(0, g, m)
+                for gq in range(g + 1):
+                    one_matmul(0, gq, g)
+            elif b == 4:
                 for m in range(M_TILES):
                     one_matmul(b, g, m)
+            elif g >= 1:
+                for gq in range(0 if g == 1 else g, g + 1):
+                    for m in range(M_TILES):
+                        one_matmul(b, gq, m)
 
         pend = {}
 
@@ -298,10 +303,12 @@ def tile_multiqueryattention_pa_kernel(tc, x, sin, cos, W_qkv_bytes, W_qkv_scale
 
         xtranspose(0)
         xtranspose(1)
-        widen_to(LOOKAHEAD)
+        for s in range(-LA_E, 0):
+            prepare(s)
         interleave(0)
         for s in range(n):
             b, g = steps[s]
+            prepare(s)
             interleave(s + 1)
             if b == 0:
                 xcopy(g, 0)
@@ -312,11 +319,13 @@ def tile_multiqueryattention_pa_kernel(tc, x, sin, cos, W_qkv_bytes, W_qkv_scale
             flush_late()
             if b == 0:
                 xquant(g)
-            matmuls(s)
             sb = s - DELAY
             if sb >= 0 and steps[sb][1] == PASSES - 1:
                 interleave(s + 2)
                 run(steps[sb][0])
+            matmuls(s)
+            if s + LA_P in PE_STEPS:
+                pe_interleave(s + LA_P)
         for sb in range(n - DELAY, n):
             if steps[sb][1] == PASSES - 1:
                 run(steps[sb][0])

@@ -29,7 +29,7 @@ BLOCKS = [(0, 512), (512, 512), (1024, 512), (1536, 512), (2048, 256)]
 GPSIMD_ADDS = {(0, 0), (0, 1), (1, 0), (1, 1), (2, 0), (2, 1), (3, 0), (3, 1)}
 PE_STEPS = {6, 7, 8, 10, 12, 14, 15}
 S_STEPS = {17, 18, 19}
-VECTOR_WIDENS = {(0, 0), (0, 2), (0, 3), (1, 1)}
+VECTOR_WIDENS = {(0, 0), (0, 2), (0, 3), (1, 1), (8, 1), (10, 1), (12, 1), (14, 1)}
 LA_W = 4
 LA_P = 4
 LA_E = 2

@@ -139,8 +139,8 @@ def tile_multiqueryattention_pa_kernel(tc, x, sin, cos, W_qkv_bytes, W_qkv_scale
                 for q in range(2):
                     c0 = (2 * h + q) * P
                     nc.tensor.matmul(
-                        out=pil[:, q * 512:(q + 1) * 512], lhsT=identb[:],
-                        rhs=wide_t[s][:, :, c0:c0 + P].rearrange("p t c -> p c t"),
+                        out=pil[:, q * 512:(q + 1) * 512].rearrange("p (c t) -> p t c", t=PACK), lhsT=identb[:],
+                        rhs=wide_t[s][:, :, c0:c0 + P],
                         start=True, stop=True,
                     )
                 halves.append(pil)

@@ -34,6 +34,7 @@ LA_W = 4
 LA_P = 4
 LA_E = 2
 DELAY = 2
+DEFER = {(0, 2), (1, 2), (2, 2)}
 LOAD_ORDER = [("w", 0), ("w", 1), ("x", 0), ("w", 2), ("x", 1), ("tab", 0), ("w", 3), ("x", 2), ("x", 3)]
 
 
@@ -130,6 +131,7 @@ def tile_multiqueryattention_pa_kernel(tc, x, sin, cos, W_qkv_bytes, W_qkv_scale
                 nc.scalar.copy(out=dst, in_=src)
             else:
                 nc.vector.tensor_copy(out=dst, in_=src)
+                state["vlast"] = ("b", grp[:, w - 1, PACK - 2:PACK])
             grp_t[s] = grp
 
         def pe_interleave(s):
@@ -182,6 +184,7 @@ def tile_multiqueryattention_pa_kernel(tc, x, sin, cos, W_qkv_bytes, W_qkv_scale
                 in_=grp_t[s][:].rearrange("p n t -> p (n t)"),
             )
             codes_t[s] = (codes, scl)
+            state["vlast"] = ("u", codes[:, w - 1:w])
 
         xt_t = {}
         xg_t = {}
@@ -276,7 +279,7 @@ def tile_multiqueryattention_pa_kernel(tc, x, sin, cos, W_qkv_bytes, W_qkv_scale
             tt = pend[(b, m)]
             nh = 4 if b < 4 else 1
             oo = epi.tile([P, nh, 2, HALF], F32, tag="oq" if b < 4 else "ok")
-            eng = nc.gpsimd if (b, m) in GPSIMD_ADDS else nc.vector
+            eng = nc.gpsimd if ((b, m) in GPSIMD_ADDS or (b, m) in DEFER) else nc.vector
             eng.tensor_tensor(out=oo[:], in0=tt[:, :, :, 0:HALF], in1=tt[:, :, :, HALF:HD], op=ALU.add)
             if b < 4:
                 nc.sync.dma_start(
@@ -287,12 +290,23 @@ def tile_multiqueryattention_pa_kernel(tc, x, sin, cos, W_qkv_bytes, W_qkv_scale
                 nc.sync.dma_start(out=out_1[0, m * P:(m + 1) * P, :], in_=oo[:].rearrange("p h w i -> p (h w i)"))
 
         late = []
+        deferred = []
+        gate_b = consts.tile([P, 2], BF16, name="gate_b")
+        gate_u = consts.tile([P, 1], U32, name="gate_u")
 
         def run(b):
+            if deferred:
+                kind, col = state["vlast"]
+                nc.gpsimd.tensor_copy(out=gate_b[:] if kind == "b" else gate_u[:], in_=col)
+                for (bb, mm) in deferred:
+                    finish(bb, mm)
+                deferred.clear()
             for m in range(M_TILES):
                 products(b, m)
                 if (b, m) in GPSIMD_ADDS:
                     finish(b, m)
+                elif (b, m) in DEFER:
+                    deferred.append((b, m))
                 else:
                     late.append((b, m))
 

@@ -34,6 +34,9 @@ LA_W = 4
 LA_P = 4
 LA_E = 2
 DELAY = 2
+S_EARLY = 0
+HOLD_LATE = 1
+LATE = {14: 1, 15: 1}
 DEFER = {(0, 2), (1, 2), (2, 2)}
 LOAD_ORDER = [("w", 0), ("w", 1), ("x", 0), ("w", 2), ("x", 1), ("tab", 0), ("w", 3), ("x", 2), ("x", 3)]
 
@@ -136,7 +139,7 @@ def tile_multiqueryattention_pa_kernel(tc, x, sin, cos, W_qkv_bytes, W_qkv_scale
 
         def pe_interleave(s):
             halves = []
-            for h in range(2):
+            for h in range(BLOCKS[steps[s][0]][1] // 256):
                 pil = psum.tile([P, 1024], BF16, tag="pil")
                 for q in range(2):
                     c0 = (2 * h + q) * P
@@ -149,9 +152,9 @@ def tile_multiqueryattention_pa_kernel(tc, x, sin, cos, W_qkv_bytes, W_qkv_scale
             pil_t[s] = halves
 
         def evacuate(s):
-            grp = grpp.tile([P, 512, PACK], BF16, tag="grp", align_bytes=64)
+            grp = grpp.tile([P, BLOCKS[steps[s][0]][1], PACK], BF16, tag="grp", align_bytes=64)
             flat = grp[:].rearrange("p n t -> p (n t)")
-            for h in range(2):
+            for h in range(len(pil_t[s])):
                 nc.scalar.copy(out=flat[:, h * 1024:(h + 1) * 1024], in_=pil_t[s][h][:])
             grp_t[s] = grp
 
@@ -160,17 +163,20 @@ def tile_multiqueryattention_pa_kernel(tc, x, sin, cos, W_qkv_bytes, W_qkv_scale
                 s = state["widened"]
                 widen(s)
                 state["widened"] = s + 1
+                if S_EARLY and s in S_STEPS:
+                    copy_interleave(s)
 
         def prepare(s):
             widen_to(s + LA_W + 1)
+            for k in sorted(PE_STEPS):
+                if k - LA_E + LATE.get(k, 0) == s:
+                    evacuate(k)
             k = s + LA_E
-            if k < n and k in PE_STEPS:
-                evacuate(k)
-            if k < n and k in S_STEPS:
+            if k < n and k in S_STEPS and not S_EARLY:
                 copy_interleave(k)
 
         def interleave(s):
-            if s < n and s not in grp_t:
+            if s < n and s not in grp_t and s not in PE_STEPS and s not in S_STEPS:
                 copy_interleave(s)
 
         def quantize(s):
@@ -330,7 +336,8 @@ def tile_multiqueryattention_pa_kernel(tc, x, sin, cos, W_qkv_bytes, W_qkv_scale
                 if g + 2 < M_TILES:
                     xtranspose(g + 2)
             quantize(s)
-            flush_late()
+            if not (HOLD_LATE and s == n - 2):
+                flush_late()
             if b == 0:
                 xquant(g)
             sb = s - DELAY
@@ -338,8 +345,9 @@ def tile_multiqueryattention_pa_kernel(tc, x, sin, cos, W_qkv_bytes, W_qkv_scale
                 interleave(s + 2)
                 run(steps[sb][0])
             matmuls(s)
-            if s + LA_P in PE_STEPS:
-                pe_interleave(s + LA_P)
+            for k in sorted(PE_STEPS):
+                if k - LA_P + LATE.get(k, 0) == s:
+                    pe_interleave(k)
         for sb in range(n - DELAY, n):
             if steps[sb][1] == PASSES - 1:
                 run(steps[sb][0])

@@ -38,7 +38,7 @@ S_EARLY = 0
 HOLD_LATE = 1
 LATE = {14: 1, 15: 1}
 DEFER = {(0, 2), (1, 2), (2, 2)}
-LOAD_ORDER = [("w", 0), ("w", 1), ("x", 0), ("w", 2), ("x", 1), ("tab", 0), ("w", 3), ("x", 2), ("x", 3)]
+LOAD_ORDER = [("w", 0), ("w", 1), ("x", 0), ("w", 2), ("x", 1), ("w", 3), ("w", 4), ("x", 2), ("w", 5), ("w", 6), ("x", 3), ("w", 7), ("tab", 0)]
 
 
 def tile_multiqueryattention_pa_kernel(tc, x, sin, cos, W_qkv_bytes, W_qkv_scale, out_0, out_1, out_2):
@@ -87,15 +87,16 @@ def tile_multiqueryattention_pa_kernel(tc, x, sin, cos, W_qkv_bytes, W_qkv_scale
 
         for item in LOAD_ORDER:
             if item[0] == "w":
-                load_w(0, item[1])
+                load_w(item[1] // PASSES, item[1] % PASSES)
             elif item[0] == "x":
                 load_x(item[1])
             else:
                 nc.sync.dma_start(out=cos_sb[:], in_=cos.rearrange("(m p) j -> p m j", p=P))
                 nc.sync.dma_start(out=sin_sb[:], in_=sin.rearrange("(m p) j -> p m j", p=P))
-        for b in range(1, len(BLOCKS)):
+        for b in range(len(BLOCKS)):
             for g in range(PASSES):
-                load_w(b, g)
+                if (b, g) not in wbytes:
+                    load_w(b, g)
 
         tabq = consts.tile([P, M_TILES, 4, HALF], F32, name="tabq")
         quarters = [(cos_sb, 0, SCALE), (sin_sb, 0, -SCALE), (sin_sb, 1, SCALE), (cos_sb, 1, SCALE)]

@@ -30,6 +30,7 @@ GPSIMD_ADDS = {(0, 0), (0, 1), (1, 0), (1, 1), (2, 0), (2, 1), (3, 0), (3, 1)}
 PE_STEPS = {6, 7, 8, 10, 12, 14, 15}
 S_STEPS = {17, 18, 19}
 VECTOR_WIDENS = {(0, 0), (0, 2), (0, 3), (1, 1), (8, 1), (10, 1), (12, 1), (14, 1)}
+KGROUP = 2
 LA_W = 4
 LA_P = 4
 LA_E = 2
@@ -257,6 +258,9 @@ def tile_multiqueryattention_pa_kernel(tc, x, sin, cos, W_qkv_bytes, W_qkv_scale
                         one_matmul(b, gq, m)
 
         pend = {}
+        tk_all = consts.tile([P, M_TILES, 2, HD], F32, name="tk_all")
+        vv_all = consts.tile([P, M_TILES, HD], F32, name="vv_all")
+        ok_all = consts.tile([P, M_TILES, 2, HALF], F32, name="ok_all")
 
         def products(b, m):
             acc = banks[(b, m)]
@@ -269,12 +273,12 @@ def tile_multiqueryattention_pa_kernel(tc, x, sin, cos, W_qkv_bytes, W_qkv_scale
                     op=ALU.mult,
                 )
             else:
-                tt = epi.tile([P, 1, 2, HD], F32, tag="tk")
-                vv = epi.tile([P, HD], F32, tag="vv")
-                nc.scalar.copy(out=vv[:], in_=acc[:, HD:2 * HD])
-                nc.sync.dma_start(out=out_2[0, m * P:(m + 1) * P, :], in_=vv[:])
+                tt = tk_all
+                nc.scalar.copy(out=vv_all[:, m, :], in_=acc[:, HD:2 * HD])
+                if m == M_TILES - 1:
+                    nc.sync.dma_start(out=out_2[0, :, :].rearrange("(m p) j -> p m j", p=P), in_=vv_all[:])
                 nc.vector.scalar_tensor_tensor(
-                    out=tt[:, 0, :, :],
+                    out=tt[:, m, :, :],
                     in0=acc[:, 0:HD].unsqueeze(1).to_broadcast([P, 2, HD]),
                     scalar=1.0 / SCALE,
                     in1=tabq[:, m, :, :].rearrange("p (w r) i -> p w (r i)", w=2),
@@ -283,6 +287,17 @@ def tile_multiqueryattention_pa_kernel(tc, x, sin, cos, W_qkv_bytes, W_qkv_scale
             pend[(b, m)] = tt
 
         def finish(b, m):
+            if b == 4:
+                if (m + 1) % KGROUP == 0:
+                    m0 = m + 1 - KGROUP
+                    nc.vector.tensor_tensor(
+                        out=ok_all[:, m0:m + 1, :, :], in0=tk_all[:, m0:m + 1, :, 0:HALF], in1=tk_all[:, m0:m + 1, :, HALF:HD], op=ALU.add,
+                    )
+                    nc.sync.dma_start(
+                        out=out_1[0, m0 * P:(m + 1) * P, :].rearrange("(m p) j -> p m j", p=P),
+                        in_=ok_all[:, m0:m + 1, :, :].rearrange("p m w i -> p m (w i)"),
+                    )
+                return
             tt = pend[(b, m)]
             nh = 4 if b < 4 else 1
             oo = epi.tile([P, nh, 2, HALF], F32, tag="oq" if b < 4 else "ok")

@@ -31,6 +31,7 @@ PE_STEPS = {6, 7, 8, 10, 12, 14, 15}
 S_STEPS = {17, 18, 19}
 VECTOR_WIDENS = {(0, 0), (0, 2), (0, 3), (1, 1), (8, 1), (10, 1), (12, 1), (14, 1)}
 KGROUP = 2
+RUN = 8
 LA_W = 4
 LA_P = 4
 LA_E = 2
@@ -130,8 +131,8 @@ def tile_multiqueryattention_pa_kernel(tc, x, sin, cos, W_qkv_bytes, W_qkv_scale
             b, g = steps[s]
             w = BLOCKS[b][1]
             grp = grpp.tile([P, w, PACK], BF16, tag="grp", align_bytes=64)
-            dst = grp[:].rearrange("p (c i) t -> p c t i", i=4)
-            src = wide_t[s][:].rearrange("p t (c i) -> p c t i", i=4)
+            dst = grp[:].rearrange("p (c i) t -> p c t i", i=RUN)
+            src = wide_t[s][:].rearrange("p t (c i) -> p c t i", i=RUN)
             if s in S_STEPS:
                 nc.scalar.copy(out=dst, in_=src)
             else:

@@ -350,8 +350,6 @@ def tile_multiqueryattention_pa_kernel(tc, x, sin, cos, W_qkv_bytes, W_qkv_scale
             if b == 0:
                 xcopy(g, 0)
                 xcopy(g, 1)
-                if g + 2 < M_TILES:
-                    xtranspose(g + 2)
             quantize(s)
             if not (HOLD_LATE and s == n - 2):
                 flush_late()
@@ -362,6 +360,8 @@ def tile_multiqueryattention_pa_kernel(tc, x, sin, cos, W_qkv_bytes, W_qkv_scale
                 interleave(s + 2)
                 run(steps[sb][0])
             matmuls(s)
+            if b == 0 and g + 2 < M_TILES:
+                xtranspose(g + 2)
             for k in sorted(PE_STEPS):
                 if k - LA_P + LATE.get(k, 0) == s:
                     pe_interleave(k)

@@ -253,10 +253,13 @@ def tile_multiqueryattention_pa_kernel(tc, x, sin, cos, W_qkv_bytes, W_qkv_scale
             elif b == 4:
                 for m in range(M_TILES):
                     one_matmul(b, g, m)
-            elif g >= 1:
-                for gq in range(0 if g == 1 else g, g + 1):
-                    for m in range(M_TILES):
+            elif g == 1:
+                for m in range(M_TILES):
+                    for gq in range(2):
                         one_matmul(b, gq, m)
+            elif g > 1:
+                for m in range(M_TILES):
+                    one_matmul(b, g, m)
 
         pend = {}
         tk_all = consts.tile([P, M_TILES, 2, HD], F32, name="tk_all")

from contextlib import ExitStack

import concourse.mybir as mybir
from concourse.masks import make_identity

F32 = mybir.dt.float32
BF16 = mybir.dt.bfloat16
U32 = mybir.dt.uint32
U8 = mybir.dt.uint8
FP8 = mybir.dt.float8_e4m3fn
FP8X4 = mybir.dt.float8_e4m3fn_x4
ALU = mybir.AluOpType
ACT = mybir.ActivationFunctionType

T = 512
D = 2048
HD = 128
HALF = 64
NQKV = D + 2 * HD
SCALE = HD ** (-0.5)
P = 128
PACK = 4
K_PASS = P * PACK
PASSES = D // K_PASS
M_TILES = T // P
FLOPS = 2 * T * D * NQKV

BLOCKS = [(0, 512), (512, 512), (1024, 512), (1536, 512), (2048, 256)]
GPSIMD_ADDS = {(0, 0), (0, 1), (1, 0), (1, 1), (2, 0), (2, 1), (3, 0), (3, 1)}
PE_STEPS = {6, 7, 8, 10, 12, 14, 15}
S_STEPS = {17, 18, 19}
VECTOR_WIDENS = {(0, 0), (0, 2), (0, 3), (1, 1), (8, 1), (10, 1), (12, 1), (14, 1)}
KGROUP = 2
RUN = 8
LA_W = 4
LA_P = 4
LA_E = 2
DELAY = 2
S_EARLY = 0
HOLD_LATE = 1
LATE = {14: 1, 15: 1}
DEFER = {(0, 2), (1, 2), (2, 2)}
LOAD_ORDER = [("w", 0), ("w", 1), ("x", 0), ("w", 2), ("x", 1), ("w", 3), ("w", 4), ("x", 2), ("w", 5), ("w", 6), ("x", 3), ("w", 7), ("tab", 0)]


def tile_multiqueryattention_pa_kernel(tc, x, sin, cos, W_qkv_bytes, W_qkv_scale, out_0, out_1, out_2):
    nc = tc.nc
    with ExitStack() as ctx:
        consts = ctx.enter_context(tc.tile_pool(name="consts", bufs=1))
        keep = ctx.enter_context(tc.tile_pool(name="keep", bufs=1))
        widep = ctx.enter_context(tc.tile_pool(name="widep", bufs=8))
        grpp = ctx.enter_context(tc.tile_pool(name="grpp", bufs=6))
        epi = ctx.enter_context(tc.tile_pool(name="epi", bufs=6))
        psum = ctx.enter_context(tc.psum_pool(name="psum", bufs=4))
        ctx.enter_context(tc.manual_schedule())

        steps = [(b, g) for b in range(len(BLOCKS)) for g in range(PASSES)]
        n = len(steps)

        warm = consts.tile([P, 2], F32, name="warm")
        nc.vector.memset(warm[:, 0:1], 0.0)
        nc.scalar.activation(out=warm[:, 1:2], in_=warm[:, 0:1], func=ACT.Copy)

        ident = consts.tile([P, P], F32, name="ident")
        make_identity(nc, ident[:])
        identb = consts.tile([P, P], BF16, name="identb")
        make_identity(nc, identb[:])

        wsc = consts.tile([P, PASSES, PACK], F32, name="wsc")
        nc.sync.dma_start(out=wsc[:], in_=W_qkv_scale.rearrange("(g p t) o -> p g (t o)", p=P, t=PACK))
        wbytes = {}
        x_sb = {}
        cos_sb = consts.tile([P, M_TILES, HD], BF16, name="cos_sb")
        sin_sb = consts.tile([P, M_TILES, HD], BF16, name="sin_sb")

        def load_w(b, g):
            c0, w = BLOCKS[b]
            wb = keep.tile([P, PACK, w], U8, name="wbytes%d_%d" % (b, g))
            nc.sync.dma_start(
                out=wb[:],
                in_=W_qkv_bytes[g * K_PASS:(g + 1) * K_PASS, c0:c0 + w].rearrange("(p t) n -> p t n", t=PACK),
            )
            wbytes[(b, g)] = wb

        def load_x(m):
            xs = keep.tile([P, D], BF16, name="x_sb%d" % m)
            nc.sync.dma_start(out=xs[:], in_=x[0, m * P:(m + 1) * P, :])
            x_sb[m] = xs

        for item in LOAD_ORDER:
            if item[0] == "w":
                load_w(item[1] // PASSES, item[1] % PASSES)
            elif item[0] == "x":
                load_x(item[1])
            else:
                nc.sync.dma_start(out=cos_sb[:], in_=cos.rearrange("(m p) j -> p m j", p=P))
                nc.sync.dma_start(out=sin_sb[:], in_=sin.rearrange("(m p) j -> p m j", p=P))
        for b in range(len(BLOCKS)):
            for g in range(PASSES):
                if (b, g) not in wbytes:
                    load_w(b, g)

        tabq = consts.tile([P, M_TILES, 4, HALF], F32, name="tabq")
        quarters = [(cos_sb, 0, SCALE), (sin_sb, 0, -SCALE), (sin_sb, 1, SCALE), (cos_sb, 1, SCALE)]
        for qi in range(4):
            src_t, hf, fac = quarters[qi]
            nc.gpsimd.tensor_scalar(
                out=tabq[:, :, qi, :], in0=src_t[:, :, hf * HALF:(hf + 1) * HALF],
                scalar1=fac, scalar2=0.0, op0=ALU.mult, op1=ALU.add,
            )

        wide_t = {}
        grp_t = {}
        pil_t = {}
        codes_t = {}
        state = {"widened": 0}

        def widen(s):
            b, g = steps[s]
            w = BLOCKS[b][1]
            wide = widep.tile([P, PACK, w], BF16, tag="wide")
            for t in range(PACK):
                src = wbytes[(b, g)][:, t, :].bitcast(FP8)
                if (s, t) in VECTOR_WIDENS:
                    nc.vector.tensor_scalar(out=wide[:, t, :], in0=src, scalar1=wsc[:, g, t:t + 1], scalar2=None, op0=ALU.mult)
                else:
                    nc.scalar.activation(out=wide[:, t, :], in_=src, func=ACT.Copy, scale=wsc[:, g, t:t + 1])
            wide_t[s] = wide

        def copy_interleave(s):
            b, g = steps[s]
            w = BLOCKS[b][1]
            grp = grpp.tile([P, w, PACK], BF16, tag="grp", align_bytes=64)
            dst = grp[:].rearrange("p (c i) t -> p c t i", i=RUN)
            src = wide_t[s][:].rearrange("p t (c i) -> p c t i", i=RUN)
            if s in S_STEPS:
                nc.scalar.copy(out=dst, in_=src)
            else:
                nc.vector.tensor_copy(out=dst, in_=src)
                state["vlast"] = ("b", grp[:, w - 1, PACK - 2:PACK])
            grp_t[s] = grp

        def pe_interleave(s):
            halves = []
            for h in range(BLOCKS[steps[s][0]][1] // 256):
                pil = psum.tile([P, 1024], BF16, tag="pil")
                for q in range(2):
                    c0 = (2 * h + q) * P
                    nc.tensor.matmul(
                        out=pil[:, q * 512:(q + 1) * 512].rearrange("p (c t) -> p t c", t=PACK), lhsT=identb[:],
                        rhs=wide_t[s][:, :, c0:c0 + P],
                        start=True, stop=True,
                    )
                halves.append(pil)
            pil_t[s] = halves

        def evacuate(s):
            grp = grpp.tile([P, BLOCKS[steps[s][0]][1], PACK], BF16, tag="grp", align_bytes=64)
            flat = grp[:].rearrange("p n t -> p (n t)")
            for h in range(len(pil_t[s])):
                nc.scalar.copy(out=flat[:, h * 1024:(h + 1) * 1024], in_=pil_t[s][h][:])
            grp_t[s] = grp

        def widen_to(k):
            while state["widened"] < min(k, n):
                s = state["widened"]
                widen(s)
                state["widened"] = s + 1
                if S_EARLY and s in S_STEPS:
                    copy_interleave(s)

        def prepare(s):
            widen_to(s + LA_W + 1)
            for k in sorted(PE_STEPS):
                if k - LA_E + LATE.get(k, 0) == s:
                    evacuate(k)
            k = s + LA_E
            if k < n and k in S_STEPS and not S_EARLY:
                copy_interleave(k)

        def interleave(s):
            if s < n and s not in grp_t and s not in PE_STEPS and s not in S_STEPS:
                copy_interleave(s)

        def quantize(s):
            b, g = steps[s]
            w = BLOCKS[b][1]
            codes = keep.tile([P, w], U32, name="wcodes%d" % s, align_bytes=64)
            scl = keep.tile([P, w], U8, name="wscl%d" % s, align_bytes=64)
            nc.vector.quantize_mx(
                out=codes[:].bitcast(FP8X4),
                scales=scl[:],
                in_=grp_t[s][:].rearrange("p n t -> p (n t)"),
            )
            codes_t[s] = (codes, scl)
            state["vlast"] = ("u", codes[:, w - 1:w])

        xt_t = {}
        xg_t = {}
        x_codes = {}

        def xtranspose(m):
            words = x_sb[m][:].bitcast(F32)
            for gp in range(PASSES // 2):
                xt = psum.tile([P, 512], F32, tag="pil")
                for gg in range(2):
                    g = 2 * gp + gg
                    for u in range(2):
                        col = (2 * gg + u) * P
                        nc.tensor.transpose(xt[:, col:col + P], words[:, 256 * g + u:256 * (g + 1):2], ident[:])
                xt_t[(m, gp)] = xt

        def xcopy(m, gp):
            if gp == 0:
                xg = keep.tile([P, PASSES, P, PACK], BF16, name="xg%d" % m, align_bytes=64)
                xg_t[m] = xg
            dst = xg_t[m][:, 2 * gp:2 * gp + 2, :, :].bitcast(F32)
            src = xt_t[(m, gp)][:].rearrange("p (g u r) -> p g r u", g=2, u=2)
            nc.vector.tensor_copy(out=dst, in_=src)

        def xquant(m):
            xc = keep.tile([P, PASSES * P], U32, name="xc%d" % m, align_bytes=64)
            xsc = keep.tile([P, PASSES * P], U8, name="xsc%d" % m, align_bytes=64)
            nc.vector.quantize_mx(out=xc[:].bitcast(FP8X4), scales=xsc[:], in_=xg_t[m][:].rearrange("p g r t -> p (g r t)"))
            x_codes[m] = (xc, xsc)

        banks = {}

        def one_matmul(b, g, m):
            w = BLOCKS[b][1]
            codes, scl = codes_t[PASSES * b + g]
            if g == 0:
                acc = psum.tile([P, 512], F32, tag="acc" if b < 4 else "pil")
                banks[(b, m)] = acc
            xc, xsc = x_codes[m]
            nc.tensor.matmul_mx(
                out=banks[(b, m)][:, 0:w],
                lhsT=xc[:, g * P:(g + 1) * P].bitcast(FP8X4),
                lhsT_scale=xsc[:, g * P:(g + 1) * P],
                rhs=codes[:].bitcast(FP8X4),
                rhs_scale=scl[:],
                start=(g == 0),
                stop=(g == PASSES - 1),
            )

        def matmuls(s):
            b, g = steps[s]
            if b == 0:
                for m in range(g):
                    one_matmul(0, g, m)
                for gq in range(g + 1):
                    one_matmul(0, gq, g)
            elif b == 4:
                for m in range(M_TILES):
                    one_matmul(b, g, m)
            elif g == 1:
                for m in range(M_TILES):
                    for gq in range(2):
                        one_matmul(b, gq, m)
            elif g > 1:
                for m in range(M_TILES):
                    one_matmul(b, g, m)

        pend = {}
        tk_all = consts.tile([P, M_TILES, 2, HD], F32, name="tk_all")
        vv_all = consts.tile([P, M_TILES, HD], F32, name="vv_all")
        ok_all = consts.tile([P, M_TILES, 2, HALF], F32, name="ok_all")

        def products(b, m):
            acc = banks[(b, m)]
            if b < 4:
                tt = epi.tile([P, 4, 2, HD], F32, tag="tt")
                nc.vector.tensor_tensor(
                    out=tt[:],
                    in0=acc[:, 0:512].rearrange("p (h j) -> p h j", h=4).unsqueeze(2).to_broadcast([P, 4, 2, HD]),
                    in1=tabq[:, m, :, :].rearrange("p (w r) i -> p w (r i)", w=2).unsqueeze(1).to_broadcast([P, 4, 2, HD]),
                    op=ALU.mult,
                )
            else:
                tt = tk_all
                nc.scalar.copy(out=vv_all[:, m, :], in_=acc[:, HD:2 * HD])
                if m == M_TILES - 1:
                    nc.sync.dma_start(out=out_2[0, :, :].rearrange("(m p) j -> p m j", p=P), in_=vv_all[:])
                nc.vector.scalar_tensor_tensor(
                    out=tt[:, m, :, :],
                    in0=acc[:, 0:HD].unsqueeze(1).to_broadcast([P, 2, HD]),
                    scalar=1.0 / SCALE,
                    in1=tabq[:, m, :, :].rearrange("p (w r) i -> p w (r i)", w=2),
                    op0=ALU.mult, op1=ALU.mult,
                )
            pend[(b, m)] = tt

        def finish(b, m):
            if b == 4:
                if (m + 1) % KGROUP == 0:
                    m0 = m + 1 - KGROUP
                    nc.vector.tensor_tensor(
                        out=ok_all[:, m0:m + 1, :, :], in0=tk_all[:, m0:m + 1, :, 0:HALF], in1=tk_all[:, m0:m + 1, :, HALF:HD], op=ALU.add,
                    )
                    nc.sync.dma_start(
                        out=out_1[0, m0 * P:(m + 1) * P, :].rearrange("(m p) j -> p m j", p=P),
                        in_=ok_all[:, m0:m + 1, :, :].rearrange("p m w i -> p m (w i)"),
                    )
                return
            tt = pend[(b, m)]
            nh = 4 if b < 4 else 1
            oo = epi.tile([P, nh, 2, HALF], F32, tag="oq" if b < 4 else "ok")
            eng = nc.gpsimd if ((b, m) in GPSIMD_ADDS or (b, m) in DEFER) else nc.vector
            eng.tensor_tensor(out=oo[:], in0=tt[:, :, :, 0:HALF], in1=tt[:, :, :, HALF:HD], op=ALU.add)
            if b < 4:
                nc.sync.dma_start(
                    out=out_0[0, 4 * b:4 * b + 4, m * P:(m + 1) * P, :].rearrange("h p j -> p h j"),
                    in_=oo[:].rearrange("p h w i -> p h (w i)"),
                )
            else:
                nc.sync.dma_start(out=out_1[0, m * P:(m + 1) * P, :], in_=oo[:].rearrange("p h w i -> p (h w i)"))

        late = []
        deferred = []
        gate_b = consts.tile([P, 2], BF16, name="gate_b")
        gate_u = consts.tile([P, 1], U32, name="gate_u")

        def run(b):
            if deferred:
                kind, col = state["vlast"]
                nc.gpsimd.tensor_copy(out=gate_b[:] if kind == "b" else gate_u[:], in_=col)
                for (bb, mm) in deferred:
                    finish(bb, mm)
                deferred.clear()
            for m in range(M_TILES):
                products(b, m)
                if (b, m) in GPSIMD_ADDS:
                    finish(b, m)
                elif (b, m) in DEFER:
                    deferred.append((b, m))
                else:
                    late.append((b, m))

        def flush_late():
            for (bb, mm) in late:
                finish(bb, mm)
            late.clear()

        xtranspose(0)
        xtranspose(1)
        for s in range(-LA_E, 0):
            prepare(s)
        interleave(0)
        for s in range(n):
            b, g = steps[s]
            prepare(s)
            interleave(s + 1)
            if b == 0:
                xcopy(g, 0)
                xcopy(g, 1)
            quantize(s)
            if not (HOLD_LATE and s == n - 2):
                flush_late()
            if b == 0:
                xquant(g)
            sb = s - DELAY
            if sb >= 0 and steps[sb][1] == PASSES - 1:
                interleave(s + 2)
                run(steps[sb][0])
            matmuls(s)
            if b == 0 and g + 2 < M_TILES:
                xtranspose(g + 2)
            for k in sorted(PE_STEPS):
                if k - LA_P + LATE.get(k, 0) == s:
                    pe_interleave(k)
        for sb in range(n - DELAY, n):
            if steps[sb][1] == PASSES - 1:
                run(steps[sb][0])
        flush_late()
